import numpy as np
import ml_dtypes


def mxq(x, axis, fmt="e4m3"):
    dtype, down = {"e4m3": (ml_dtypes.float8_e4m3fn, 7), "e5m2": (ml_dtypes.float8_e5m2, 14)}[fmt]
    v = np.moveaxis(np.asarray(x, np.float32).astype(ml_dtypes.bfloat16).astype(np.float64), axis, -1)
    blocks = v.reshape(v.shape[:-1] + (-1, 32))
    amax = np.abs(blocks).max(-1, keepdims=True)
    byte = np.maximum(np.where(amax > 0, np.frexp(amax)[1] - 1 + 127, 0) - down, 1)
    scale = np.exp2(byte - 127.0)
    codes = (blocks / scale).astype(np.float32).astype(dtype).astype(np.float64)
    return np.moveaxis((codes * scale).reshape(v.shape), -1, axis)


WIDE = False


def mx_kscale(k):
    if not WIDE:
        return np.ones(k)
    levels = np.array([10, -10, 5, -5, 0])
    a = np.random.permutation(np.resize(levels, k // 512 * 4)).reshape(k // 512, 4)
    idx = np.arange(k)
    return np.exp2(a[idx // 512, idx % 128 // 32])


BF16 = ml_dtypes.bfloat16


def bf(x):
    return np.asarray(x, np.float32).astype(BF16)


def f64(x):
    return np.asarray(x).astype(np.float64)


B, S, D_IN, D_OUT = 4, 2048, 1024, 256
THRESHOLD = 2.0 / 3.0


def _quantize_1_58_bit(weight):
    scale = np.clip(np.mean(np.abs(weight)), 1e-5, 1000.0)
    weight_norm = np.clip(weight / scale, -10.0, 10.0)
    q = np.where(weight_norm > THRESHOLD, 1.0, np.where(weight_norm < -THRESHOLD, -1.0, 0.0))
    return q, scale


def setup_inputs():
    s = mx_kscale(D_IN)
    r = 1.0 / s**2
    keep = r >= 0.5 * np.mean(r)
    g = np.exp2(np.round(-np.log2(np.mean(r) * np.sqrt(np.mean(keep * s**2)))))
    return {"x": bf(np.random.standard_normal((B, S, D_IN)) * s),
            "weight": bf(np.random.standard_normal((D_OUT, D_IN)) * 1.5 / np.sqrt(D_IN) * r * g),
            "bias": bf(np.random.standard_normal(D_OUT) * 0.1)}


def reference(x, weight, bias):
    q, scale = _quantize_1_58_bit(f64(weight))
    weight_q = q * scale
    out = (mxq(f64(x), 2, "e4m3") @ mxq(weight_q, 1, "e4m3").T) + f64(bias)
    return out

@@ -1,0 +1,192 @@
+from contextlib import ExitStack
+
+import concourse.mybir as mybir
+from concourse.masks import make_identity
+
+F32 = mybir.dt.float32
+BF16 = mybir.dt.bfloat16
+U32 = mybir.dt.uint32
+U8 = mybir.dt.uint8
+FP8X4 = mybir.dt.float8_e4m3fn_x4
+ALU = mybir.AluOpType
+ACT = mybir.ActivationFunctionType
+
+P = 128
+TOKENS = 4 * 2048
+D_IN = 1024
+D_OUT = 256
+FLOPS = 2 * TOKENS * D_IN * D_OUT
+
+T = 4
+CHUNK = P * T
+NR = TOKENS // CHUNK
+NXB = 10
+NOB = 12
+WORDS = D_IN // 2
+
+
+def tile_bitnetlinear_t_kernel(tc, x, weight, bias, out):
+    nc = tc.nc
+    xf = x.flatten_outer_dims()
+    of = out.flatten_outer_dims()
+
+    with ExitStack() as ctx:
+        const = ctx.enter_context(tc.tile_pool(name="const", bufs=1))
+        xpool = ctx.enter_context(tc.tile_pool(name="xin", bufs=NXB))
+        gpool = ctx.enter_context(tc.tile_pool(name="grouped", bufs=3))
+        cpool = ctx.enter_context(tc.tile_pool(name="codes", bufs=5))
+        opool = ctx.enter_context(tc.tile_pool(name="outs", bufs=NOB))
+        ps_t = ctx.enter_context(tc.psum_pool(name="ps_t", bufs=4))
+        ps_o = ctx.enter_context(tc.psum_pool(name="ps_o", bufs=4))
+        ctx.enter_context(tc.manual_schedule())
+
+        x_tiles = {}
+
+        def load(c):
+            x_sb = xpool.tile([P, T * D_IN], BF16, name="x_sb", tag="x_sb")
+            nc.sync.dma_start(
+                out=x_sb[:],
+                in_=xf[c * CHUNK : (c + 1) * CHUNK, :].rearrange("(p t) k -> p (t k)", t=T),
+            )
+            x_tiles[c] = x_sb
+
+        w_sb = const.tile([P, 2 * D_IN], BF16, name="w_sb")
+        nc.sync.dma_start(
+            out=w_sb[:].rearrange("p (a k) -> p a k", a=2),
+            in_=weight.rearrange("(a p) k -> p a k", a=2),
+        )
+        for c in range(NXB):
+            load(c)
+
+        ones_mean = const.tile([P, P], F32, name="ones_mean")
+        nc.vector.memset(ones_mean[:], 1.0 / (D_OUT * D_IN))
+        bias_rows = const.tile([P, D_OUT], BF16, name="bias_rows")
+        nc.vector.memset(bias_rows[:], 0.0)
+        ones_bf = const.tile([P, P], BF16, name="ones_bf")
+        nc.vector.memset(ones_bf[:], 1.0)
+        nc.scalar.dma_start(out=bias_rows[0:1, :], in_=bias.unsqueeze(0))
+        warm = const.tile([P, 1], F32, name="warm")
+        nc.scalar.activation(out=warm[:], in_=ones_mean[:, 0:1], func=ACT.Abs)
+        ident = const.tile([P, P], F32, name="ident")
+        make_identity(nc, ident[:])
+
+        def transposes(src_words, name):
+            tp = ps_t.tile([P, 512], F32, name=name, tag="tp")
+            for j in range(4):
+                nc.tensor.transpose(
+                    tp[:, j * P : (j + 1) * P], src_words[:, j * P : (j + 1) * P], ident[:]
+                )
+            return tp[:].rearrange("p (g u c) -> p g c u", g=2, u=2, c=P)
+
+        ww = w_sb[:].bitcast(F32)
+        wg = const.tile([P, 2 * D_IN], BF16, name="wg", align_bytes=64)
+        wg32 = wg[:].bitcast(F32).rearrange("p (g a c u) -> p a g c u", g=2, a=2, c=P, u=2)
+        abs_sum = const.tile([P, 1], F32, name="abs_sum")
+        abs_junk = const.tile([P, 2 * D_IN], BF16, name="abs_junk")
+        nc.scalar.activation(out=abs_junk[:], in_=w_sb[:], func=ACT.Abs, accum_out=abs_sum[:])
+        for a in range(2):
+            tpw = transposes(ww[:, a * WORDS : (a + 1) * WORDS], "tpw")
+            nc.vector.tensor_copy(out=wg32[:, a], in_=tpw)
+
+        bias_ps = ps_o.tile([P, 512], F32, name="bias_ps", tag="op")
+        for h in range(2):
+            nc.tensor.matmul(
+                out=bias_ps[:, h * D_OUT : (h + 1) * D_OUT],
+                lhsT=ones_bf[:],
+                rhs=bias_rows[:],
+                start=True,
+                stop=True,
+            )
+        bias2 = const.tile([P, 512], F32, name="bias2")
+        nc.vector.tensor_copy(out=bias2[:], in_=bias_ps[:])
+
+        mean_ps = ps_o.tile([P, 512], F32, name="mean_ps", tag="op")
+        nc.tensor.matmul(
+            out=mean_ps[:, 0:1], lhsT=ones_mean[:], rhs=abs_sum[:], start=True, stop=True
+        )
+        sv = const.tile([P, 4], F32, name="sv")
+        scale = sv[:, 0:1]
+        thr = sv[:, 1:2]
+        nthr = sv[:, 2:3]
+        nc.vector.tensor_scalar(
+            out=scale, in0=mean_ps[:, 0:1], scalar1=1e-5, scalar2=1000.0, op0=ALU.max, op1=ALU.min
+        )
+        nc.vector.tensor_scalar(out=thr, in0=scale, scalar1=2.0 / 3.0, scalar2=None, op0=ALU.mult)
+        nc.vector.tensor_scalar(out=nthr, in0=scale, scalar1=-2.0 / 3.0, scalar2=None, op0=ALU.mult)
+        w_pos = const.tile([P, 2 * D_IN], BF16, name="w_pos")
+        w_neg = const.tile([P, 2 * D_IN], BF16, name="w_neg")
+        wq = const.tile([P, 2 * D_IN], BF16, name="wq", align_bytes=64)
+        nc.vector.tensor_scalar(
+            out=w_pos[:], in0=wg[:], scalar1=thr, scalar2=scale, op0=ALU.is_gt, op1=ALU.mult
+        )
+        nc.vector.tensor_scalar(
+            out=w_neg[:], in0=wg[:], scalar1=nthr, scalar2=scale, op0=ALU.is_lt, op1=ALU.mult
+        )
+        nc.vector.tensor_tensor(out=wq[:], in0=w_pos[:], in1=w_neg[:], op=ALU.subtract)
+        w_codes = const.tile([P, 2 * D_OUT], U32, name="w_codes", align_bytes=64)
+        w_scales = const.tile([P, 2 * D_OUT], U8, name="w_scales", align_bytes=64)
+        nc.vector.quantize_mx(out=w_codes[:].bitcast(FP8X4), scales=w_scales[:], in_=wq[:])
+
+        grouped = {}
+        codes = {}
+        outs = {}
+
+        def stage_t(c):
+            xw = x_tiles[c][:].bitcast(F32)
+            gr = gpool.tile([P, T * D_IN], BF16, name="gr", tag="gr", align_bytes=64)
+            gr32 = gr[:].bitcast(F32).rearrange("p (t g c u) -> p t g c u", t=T, g=2, c=P, u=2)
+            for t in range(T):
+                tp = transposes(xw[:, t * WORDS : (t + 1) * WORDS], "tp")
+                nc.scalar.copy(out=gr32[:, t], in_=tp)
+            grouped[c] = gr
+
+        def stage_q(c):
+            cd = cpool.tile([P, T * 2 * P], U32, name="cd", tag="cd", align_bytes=64)
+            sc = cpool.tile([P, T * 2 * P], U8, name="sc", tag="sc", align_bytes=64)
+            nc.vector.quantize_mx(out=cd[:].bitcast(FP8X4), scales=sc[:], in_=grouped[c][:])
+            codes[c] = (cd, sc)
+
+        def stage_m(c):
+            cd, sc = codes[c]
+            osb = opool.tile([P, T * D_OUT], F32, name="osb", tag="osb")
+            for h in range(T // 2):
+                op = ps_o.tile([P, 512], F32, name="op", tag="op")
+                for i in range(2):
+                    t = 2 * h + i
+                    for g in range(2):
+                        cols = slice((2 * t + g) * P, (2 * t + g + 1) * P)
+                        wcols = slice(g * D_OUT, (g + 1) * D_OUT)
+                        nc.tensor.matmul_mx(
+                            out=op[:, i * D_OUT : (i + 1) * D_OUT],
+                            lhsT=cd[:, cols].bitcast(FP8X4),
+                            lhsT_scale=sc[:, cols],
+                            rhs=w_codes[:, wcols].bitcast(FP8X4),
+                            rhs_scale=w_scales[:, wcols],
+                            start=(g == 0),
+                            stop=(g == 1),
+                        )
+                nc.vector.tensor_tensor(
+                    out=osb[:, h * 512 : (h + 1) * 512], in0=op[:], in1=bias2[:], op=ALU.add
+                )
+            outs[c] = osb
+
+        def store(c):
+            nc.sync.dma_start(
+                out=of[c * CHUNK : (c + 1) * CHUNK, :].rearrange("(p t) o -> p (t o)", t=T),
+                in_=outs[c][:],
+            )
+
+        next_store = 0
+        for s in range(NR + 2):
+            if s < NR:
+                stage_t(s)
+                if s + NXB < NR:
+                    load(s + NXB)
+            if 1 <= s <= NR:
+                stage_q(s - 1)
+            if s >= 2:
+                stage_m(s - 2)
+                if s + NXB >= NR - 1:
+                    while next_store <= s - 2:
+                        store(next_store)
+                        next_store += 1

@@ -50,6 +50,9 @@ def tile_bitnetlinear_t_kernel(tc, x, weight, bias, out):
             )
             x_tiles[c] = x_sb
 
+        bias_rows = const.tile([P, D_OUT], BF16, name="bias_rows")
+        nc.vector.memset(bias_rows[:], 0.0)
+        nc.sync.dma_start(out=bias_rows[0:1, :], in_=bias.unsqueeze(0))
         w_sb = const.tile([P, 2 * D_IN], BF16, name="w_sb")
         nc.sync.dma_start(
             out=w_sb[:].rearrange("p (a k) -> p a k", a=2),
@@ -60,11 +63,8 @@ def tile_bitnetlinear_t_kernel(tc, x, weight, bias, out):
 
         ones_mean = const.tile([P, P], F32, name="ones_mean")
         nc.vector.memset(ones_mean[:], 1.0 / (D_OUT * D_IN))
-        bias_rows = const.tile([P, D_OUT], BF16, name="bias_rows")
-        nc.vector.memset(bias_rows[:], 0.0)
         ones_bf = const.tile([P, P], BF16, name="ones_bf")
         nc.vector.memset(ones_bf[:], 1.0)
-        nc.scalar.dma_start(out=bias_rows[0:1, :], in_=bias.unsqueeze(0))
         warm = const.tile([P, 1], F32, name="warm")
         nc.scalar.activation(out=warm[:], in_=ones_mean[:, 0:1], func=ACT.Abs)
         ident = const.tile([P, P], F32, name="ident")

@@ -16,13 +16,22 @@ TOKENS = 4 * 2048
 D_IN = 1024
 D_OUT = 256
 FLOPS = 2 * TOKENS * D_IN * D_OUT
-
-T = 4
-CHUNK = P * T
-NR = TOKENS // CHUNK
-NXB = 10
-NOB = 12
 WORDS = D_IN // 2
+
+RT = 16
+REGION = P * RT
+NREG = TOKENS // REGION
+T = 4
+NR = TOKENS // (P * T)
+RPR = RT // T
+LOADS = (
+    ((0, 4), (4, 8), (8, 12), (12, 16)),
+    ((0, 8), (8, 16)),
+    ((0, 8), (8, 16)),
+    ((0, 8), (8, 16)),
+)
+STORES = (((0, 16),), ((0, 16),), ((0, 16),), ((0, 8), (8, 12), (12, 16)))
+NXB = 3
 
 
 def tile_bitnetlinear_t_kernel(tc, x, weight, bias, out):
@@ -34,32 +43,39 @@ def tile_bitnetlinear_t_kernel(tc, x, weight, bias, out):
         const = ctx.enter_context(tc.tile_pool(name="const", bufs=1))
         xpool = ctx.enter_context(tc.tile_pool(name="xin", bufs=NXB))
         gpool = ctx.enter_context(tc.tile_pool(name="grouped", bufs=3))
-        cpool = ctx.enter_context(tc.tile_pool(name="codes", bufs=5))
-        opool = ctx.enter_context(tc.tile_pool(name="outs", bufs=NOB))
+        cpool = ctx.enter_context(tc.tile_pool(name="codes", bufs=3))
+        opool = ctx.enter_context(tc.tile_pool(name="outs", bufs=NREG))
         ps_t = ctx.enter_context(tc.psum_pool(name="ps_t", bufs=4))
         ps_o = ctx.enter_context(tc.psum_pool(name="ps_o", bufs=4))
         ctx.enter_context(tc.manual_schedule())
 
         x_tiles = {}
 
-        def load(c):
-            x_sb = xpool.tile([P, T * D_IN], BF16, name="x_sb", tag="x_sb")
+        def load(r, piece):
+            if piece == 0:
+                x_tiles[r] = xpool.tile([P, RT * D_IN], BF16, name="x_sb", tag="x_sb")
+            t0, t1 = LOADS[r][piece]
             nc.sync.dma_start(
-                out=x_sb[:],
-                in_=xf[c * CHUNK : (c + 1) * CHUNK, :].rearrange("(p t) k -> p (t k)", t=T),
+                out=x_tiles[r][:].rearrange("p (t k) -> p t k", t=RT)[:, t0:t1, :],
+                in_=xf[r * REGION : (r + 1) * REGION, :].rearrange("(p t) k -> p t k", t=RT)[
+                    :, t0:t1, :
+                ],
             )
-            x_tiles[c] = x_sb
 
         bias_rows = const.tile([P, D_OUT], BF16, name="bias_rows")
         nc.vector.memset(bias_rows[:], 0.0)
-        nc.sync.dma_start(out=bias_rows[0:1, :], in_=bias.unsqueeze(0))
         w_sb = const.tile([P, 2 * D_IN], BF16, name="w_sb")
         nc.sync.dma_start(
             out=w_sb[:].rearrange("p (a k) -> p a k", a=2),
             in_=weight.rearrange("(a p) k -> p a k", a=2),
         )
-        for c in range(NXB):
-            load(c)
+        load(0, 0)
+        nc.sync.dma_start(out=bias_rows[0:1, :], in_=bias.unsqueeze(0))
+        for piece in range(1, len(LOADS[0])):
+            load(0, piece)
+        for r in range(1, NXB):
+            for piece in range(len(LOADS[r])):
+                load(r, piece)
 
         ones_mean = const.tile([P, P], F32, name="ones_mean")
         nc.vector.memset(ones_mean[:], 1.0 / (D_OUT * D_IN))
@@ -82,23 +98,12 @@ def tile_bitnetlinear_t_kernel(tc, x, weight, bias, out):
         wg = const.tile([P, 2 * D_IN], BF16, name="wg", align_bytes=64)
         wg32 = wg[:].bitcast(F32).rearrange("p (g a c u) -> p a g c u", g=2, a=2, c=P, u=2)
         abs_sum = const.tile([P, 1], F32, name="abs_sum")
-        abs_junk = const.tile([P, 2 * D_IN], BF16, name="abs_junk")
-        nc.scalar.activation(out=abs_junk[:], in_=w_sb[:], func=ACT.Abs, accum_out=abs_sum[:])
+        w_pos = const.tile([P, 2 * D_IN], BF16, name="w_pos")
+        w_neg = const.tile([P, 2 * D_IN], BF16, name="w_neg")
+        nc.scalar.activation(out=w_pos[:], in_=w_sb[:], func=ACT.Abs, accum_out=abs_sum[:])
         for a in range(2):
             tpw = transposes(ww[:, a * WORDS : (a + 1) * WORDS], "tpw")
             nc.vector.tensor_copy(out=wg32[:, a], in_=tpw)
-
-        bias_ps = ps_o.tile([P, 512], F32, name="bias_ps", tag="op")
-        for h in range(2):
-            nc.tensor.matmul(
-                out=bias_ps[:, h * D_OUT : (h + 1) * D_OUT],
-                lhsT=ones_bf[:],
-                rhs=bias_rows[:],
-                start=True,
-                stop=True,
-            )
-        bias2 = const.tile([P, 512], F32, name="bias2")
-        nc.vector.tensor_copy(out=bias2[:], in_=bias_ps[:])
 
         mean_ps = ps_o.tile([P, 512], F32, name="mean_ps", tag="op")
         nc.tensor.matmul(
@@ -113,8 +118,6 @@ def tile_bitnetlinear_t_kernel(tc, x, weight, bias, out):
         )
         nc.vector.tensor_scalar(out=thr, in0=scale, scalar1=2.0 / 3.0, scalar2=None, op0=ALU.mult)
         nc.vector.tensor_scalar(out=nthr, in0=scale, scalar1=-2.0 / 3.0, scalar2=None, op0=ALU.mult)
-        w_pos = const.tile([P, 2 * D_IN], BF16, name="w_pos")
-        w_neg = const.tile([P, 2 * D_IN], BF16, name="w_neg")
         wq = const.tile([P, 2 * D_IN], BF16, name="wq", align_bytes=64)
         nc.vector.tensor_scalar(
             out=w_pos[:], in0=wg[:], scalar1=thr, scalar2=scale, op0=ALU.is_gt, op1=ALU.mult
@@ -126,29 +129,46 @@ def tile_bitnetlinear_t_kernel(tc, x, weight, bias, out):
         w_codes = const.tile([P, 2 * D_OUT], U32, name="w_codes", align_bytes=64)
         w_scales = const.tile([P, 2 * D_OUT], U8, name="w_scales", align_bytes=64)
         nc.vector.quantize_mx(out=w_codes[:].bitcast(FP8X4), scales=w_scales[:], in_=wq[:])
+        bias2 = const.tile([P, 512], F32, name="bias2")
+
+        def spread_bias():
+            bias_ps = ps_o.tile([P, 512], F32, name="bias_ps", tag="op")
+            for h in range(2):
+                nc.tensor.matmul(
+                    out=bias_ps[:, h * D_OUT : (h + 1) * D_OUT],
+                    lhsT=ones_bf[:],
+                    rhs=bias_rows[:],
+                    start=True,
+                    stop=True,
+                )
+            nc.vector.tensor_copy(out=bias2[:], in_=bias_ps[:])
 
         grouped = {}
         codes = {}
         outs = {}
 
-        def stage_t(c):
-            xw = x_tiles[c][:].bitcast(F32)
+        def stage_t(s):
+            r, t0 = s // RPR, (s % RPR) * T
+            xw = x_tiles[r][:].bitcast(F32)
             gr = gpool.tile([P, T * D_IN], BF16, name="gr", tag="gr", align_bytes=64)
             gr32 = gr[:].bitcast(F32).rearrange("p (t g c u) -> p t g c u", t=T, g=2, c=P, u=2)
             for t in range(T):
-                tp = transposes(xw[:, t * WORDS : (t + 1) * WORDS], "tp")
+                tp = transposes(xw[:, (t0 + t) * WORDS : (t0 + t + 1) * WORDS], "tp")
                 nc.scalar.copy(out=gr32[:, t], in_=tp)
-            grouped[c] = gr
+            grouped[s] = gr
 
-        def stage_q(c):
+        def stage_q(s):
             cd = cpool.tile([P, T * 2 * P], U32, name="cd", tag="cd", align_bytes=64)
             sc = cpool.tile([P, T * 2 * P], U8, name="sc", tag="sc", align_bytes=64)
-            nc.vector.quantize_mx(out=cd[:].bitcast(FP8X4), scales=sc[:], in_=grouped[c][:])
-            codes[c] = (cd, sc)
+            nc.vector.quantize_mx(out=cd[:].bitcast(FP8X4), scales=sc[:], in_=grouped[s][:])
+            codes[s] = (cd, sc)
 
-        def stage_m(c):
-            cd, sc = codes[c]
-            osb = opool.tile([P, T * D_OUT], F32, name="osb", tag="osb")
+        def stage_m(s):
+            r, t0 = s // RPR, (s % RPR) * T
+            cd, sc = codes[s]
+            if t0 == 0:
+                outs[r] = opool.tile([P, RT * D_OUT], F32, name="osb", tag="osb")
+            osb = outs[r]
             for h in range(T // 2):
                 op = ps_o.tile([P, 512], F32, name="op", tag="op")
                 for i in range(2):
@@ -165,28 +185,28 @@ def tile_bitnetlinear_t_kernel(tc, x, weight, bias, out):
                             start=(g == 0),
                             stop=(g == 1),
                         )
+                first = (t0 + 2 * h) * D_OUT
                 nc.vector.tensor_tensor(
-                    out=osb[:, h * 512 : (h + 1) * 512], in0=op[:], in1=bias2[:], op=ALU.add
+                    out=osb[:, first : first + 512], in0=op[:], in1=bias2[:], op=ALU.add
                 )
-            outs[c] = osb
+            for s0, s1 in STORES[r]:
+                if s1 == t0 + T:
+                    nc.sync.dma_start(
+                        out=of[r * REGION : (r + 1) * REGION, :].rearrange(
+                            "(p t) o -> p t o", t=RT
+                        )[:, s0:s1, :],
+                        in_=osb[:].rearrange("p (t o) -> p t o", t=RT)[:, s0:s1, :],
+                    )
 
-        def store(c):
-            nc.sync.dma_start(
-                out=of[c * CHUNK : (c + 1) * CHUNK, :].rearrange("(p t) o -> p (t o)", t=T),
-                in_=outs[c][:],
-            )
-
-        next_store = 0
         for s in range(NR + 2):
             if s < NR:
                 stage_t(s)
-                if s + NXB < NR:
-                    load(s + NXB)
+                if s == 0:
+                    spread_bias()
+                if (s + 1) % RPR == 0 and (s + 1) // RPR + NXB - 1 < NREG:
+                    for piece in range(len(LOADS[(s + 1) // RPR + NXB - 1])):
+                        load((s + 1) // RPR + NXB - 1, piece)
             if 1 <= s <= NR:
                 stage_q(s - 1)
             if s >= 2:
                 stage_m(s - 2)
-                if s + NXB >= NR - 1:
-                    while next_store <= s - 2:
-                        store(next_store)
-                        next_store += 1

@@ -25,7 +25,7 @@ T = 4
 NR = TOKENS // (P * T)
 RPR = RT // T
 LOADS = (
-    ((0, 4), (4, 8), (8, 12), (12, 16)),
+    ((0, 2), (2, 4), (4, 8), (8, 16)),
     ((0, 8), (8, 16)),
     ((0, 8), (8, 16)),
     ((0, 8), (8, 16)),
@@ -65,13 +65,14 @@ def tile_bitnetlinear_t_kernel(tc, x, weight, bias, out):
         bias_rows = const.tile([P, D_OUT], BF16, name="bias_rows")
         nc.vector.memset(bias_rows[:], 0.0)
         w_sb = const.tile([P, 2 * D_IN], BF16, name="w_sb")
+        load(0, 0)
         nc.sync.dma_start(
             out=w_sb[:].rearrange("p (a k) -> p a k", a=2),
             in_=weight.rearrange("(a p) k -> p a k", a=2),
         )
-        load(0, 0)
+        load(0, 1)
         nc.sync.dma_start(out=bias_rows[0:1, :], in_=bias.unsqueeze(0))
-        for piece in range(1, len(LOADS[0])):
+        for piece in range(2, len(LOADS[0])):
             load(0, piece)
         for r in range(1, NXB):
             for piece in range(len(LOADS[r])):
@@ -94,21 +95,64 @@ def tile_bitnetlinear_t_kernel(tc, x, weight, bias, out):
                 )
             return tp[:].rearrange("p (g u c) -> p g c u", g=2, u=2, c=P)
 
+        grouped = {}
+        codes = {}
+        outs = {}
+
+        def open_tiles(s):
+            gr = gpool.tile([P, T * D_IN], BF16, name="gr", tag="gr", align_bytes=64)
+            grouped[s] = gr
+
+        def transpose_tiles(s, t_from, t_to):
+            r, t0 = s // RPR, (s % RPR) * T
+            xw = x_tiles[r][:].bitcast(F32)
+            gr32 = grouped[s][:].bitcast(F32).rearrange(
+                "p (t g c u) -> p t g c u", t=T, g=2, c=P, u=2
+            )
+            for t in range(t_from, t_to):
+                tp = transposes(xw[:, (t0 + t) * WORDS : (t0 + t + 1) * WORDS], "tp")
+                nc.scalar.copy(out=gr32[:, t], in_=tp)
+
+        def stage_q(s):
+            cd = cpool.tile([P, T * 2 * P], U32, name="cd", tag="cd", align_bytes=64)
+            sc = cpool.tile([P, T * 2 * P], U8, name="sc", tag="sc", align_bytes=64)
+            nc.vector.quantize_mx(out=cd[:].bitcast(FP8X4), scales=sc[:], in_=grouped[s][:])
+            codes[s] = (cd, sc)
+
         ww = w_sb[:].bitcast(F32)
         wg = const.tile([P, 2 * D_IN], BF16, name="wg", align_bytes=64)
         wg32 = wg[:].bitcast(F32).rearrange("p (g a c u) -> p a g c u", g=2, a=2, c=P, u=2)
-        abs_sum = const.tile([P, 1], F32, name="abs_sum")
+        sum_s = const.tile([P, 1], F32, name="sum_s")
+        sum_v = const.tile([P, 1], F32, name="sum_v")
         w_pos = const.tile([P, 2 * D_IN], BF16, name="w_pos")
         w_neg = const.tile([P, 2 * D_IN], BF16, name="w_neg")
-        nc.scalar.activation(out=w_pos[:], in_=w_sb[:], func=ACT.Abs, accum_out=abs_sum[:])
+
+        open_tiles(0)
+        transpose_tiles(0, 0, 2)
+
+        nc.scalar.activation(
+            out=w_pos[:, :D_IN], in_=w_sb[:, :D_IN], func=ACT.Abs, accum_out=sum_s[:]
+        )
+        nc.vector.tensor_reduce(
+            out=sum_v[:],
+            in_=w_sb[:, D_IN:],
+            axis=mybir.AxisListType.X,
+            op=ALU.add,
+            apply_absolute_value=True,
+        )
         for a in range(2):
             tpw = transposes(ww[:, a * WORDS : (a + 1) * WORDS], "tpw")
             nc.vector.tensor_copy(out=wg32[:, a], in_=tpw)
 
         mean_ps = ps_o.tile([P, 512], F32, name="mean_ps", tag="op")
         nc.tensor.matmul(
-            out=mean_ps[:, 0:1], lhsT=ones_mean[:], rhs=abs_sum[:], start=True, stop=True
+            out=mean_ps[:, 0:1], lhsT=ones_mean[:], rhs=sum_v[:], start=True, stop=False
         )
+        nc.tensor.matmul(
+            out=mean_ps[:, 0:1], lhsT=ones_mean[:], rhs=sum_s[:], start=False, stop=True
+        )
+        transpose_tiles(0, 2, T)
+
         sv = const.tile([P, 4], F32, name="sv")
         scale = sv[:, 0:1]
         thr = sv[:, 1:2]
@@ -125,43 +169,22 @@ def tile_bitnetlinear_t_kernel(tc, x, weight, bias, out):
         nc.vector.tensor_scalar(
             out=w_neg[:], in0=wg[:], scalar1=nthr, scalar2=scale, op0=ALU.is_lt, op1=ALU.mult
         )
+        stage_q(0)
         nc.vector.tensor_tensor(out=wq[:], in0=w_pos[:], in1=w_neg[:], op=ALU.subtract)
+        bias_ps = ps_o.tile([P, 512], F32, name="bias_ps", tag="op")
+        for h in range(2):
+            nc.tensor.matmul(
+                out=bias_ps[:, h * D_OUT : (h + 1) * D_OUT],
+                lhsT=ones_bf[:],
+                rhs=bias_rows[:],
+                start=True,
+                stop=True,
+            )
+        bias2 = const.tile([P, 512], F32, name="bias2")
+        nc.vector.tensor_copy(out=bias2[:], in_=bias_ps[:])
         w_codes = const.tile([P, 2 * D_OUT], U32, name="w_codes", align_bytes=64)
         w_scales = const.tile([P, 2 * D_OUT], U8, name="w_scales", align_bytes=64)
         nc.vector.quantize_mx(out=w_codes[:].bitcast(FP8X4), scales=w_scales[:], in_=wq[:])
-        bias2 = const.tile([P, 512], F32, name="bias2")
-
-        def spread_bias():
-            bias_ps = ps_o.tile([P, 512], F32, name="bias_ps", tag="op")
-            for h in range(2):
-                nc.tensor.matmul(
-                    out=bias_ps[:, h * D_OUT : (h + 1) * D_OUT],
-                    lhsT=ones_bf[:],
-                    rhs=bias_rows[:],
-                    start=True,
-                    stop=True,
-                )
-            nc.vector.tensor_copy(out=bias2[:], in_=bias_ps[:])
-
-        grouped = {}
-        codes = {}
-        outs = {}
-
-        def stage_t(s):
-            r, t0 = s // RPR, (s % RPR) * T
-            xw = x_tiles[r][:].bitcast(F32)
-            gr = gpool.tile([P, T * D_IN], BF16, name="gr", tag="gr", align_bytes=64)
-            gr32 = gr[:].bitcast(F32).rearrange("p (t g c u) -> p t g c u", t=T, g=2, c=P, u=2)
-            for t in range(T):
-                tp = transposes(xw[:, (t0 + t) * WORDS : (t0 + t + 1) * WORDS], "tp")
-                nc.scalar.copy(out=gr32[:, t], in_=tp)
-            grouped[s] = gr
-
-        def stage_q(s):
-            cd = cpool.tile([P, T * 2 * P], U32, name="cd", tag="cd", align_bytes=64)
-            sc = cpool.tile([P, T * 2 * P], U8, name="sc", tag="sc", align_bytes=64)
-            nc.vector.quantize_mx(out=cd[:].bitcast(FP8X4), scales=sc[:], in_=grouped[s][:])
-            codes[s] = (cd, sc)
 
         def stage_m(s):
             r, t0 = s // RPR, (s % RPR) * T
@@ -198,15 +221,14 @@ def tile_bitnetlinear_t_kernel(tc, x, weight, bias, out):
                         in_=osb[:].rearrange("p (t o) -> p t o", t=RT)[:, s0:s1, :],
                     )
 
-        for s in range(NR + 2):
+        for s in range(1, NR + 2):
             if s < NR:
-                stage_t(s)
-                if s == 0:
-                    spread_bias()
+                open_tiles(s)
+                transpose_tiles(s, 0, T)
                 if (s + 1) % RPR == 0 and (s + 1) // RPR + NXB - 1 < NREG:
                     for piece in range(len(LOADS[(s + 1) // RPR + NXB - 1])):
                         load((s + 1) // RPR + NXB - 1, piece)
-            if 1 <= s <= NR:
+            if 2 <= s <= NR:
                 stage_q(s - 1)
             if s >= 2:
                 stage_m(s - 2)

@@ -22,15 +22,18 @@ RT = 16
 REGION = P * RT
 NREG = TOKENS // REGION
 T = 4
-NR = TOKENS // (P * T)
-RPR = RT // T
+ROUNDS = [(r, t0, T) for r in range(NREG) for t0 in range(0, RT, T)][:-1] + [
+    (NREG - 1, RT - 4, 2),
+    (NREG - 1, RT - 2, 2),
+]
+NR = len(ROUNDS)
 LOADS = (
-    ((0, 2), (2, 4), (4, 8), (8, 16)),
+    ((0, 2), (2, 4), (4, 8), (8, 12), (12, 16)),
     ((0, 8), (8, 16)),
     ((0, 8), (8, 16)),
     ((0, 8), (8, 16)),
 )
-STORES = (((0, 16),), ((0, 16),), ((0, 16),), ((0, 8), (8, 12), (12, 16)))
+STORES = (((0, 16),), ((0, 16),), ((0, 16),), ((0, 8), (8, 12), (12, 14), (14, 16)))
 NXB = 3
 
 
@@ -66,13 +69,12 @@ def tile_bitnetlinear_t_kernel(tc, x, weight, bias, out):
         nc.vector.memset(bias_rows[:], 0.0)
         w_sb = const.tile([P, 2 * D_IN], BF16, name="w_sb")
         load(0, 0)
+        nc.sync.dma_start(out=bias_rows[0:1, :], in_=bias.unsqueeze(0))
         nc.sync.dma_start(
             out=w_sb[:].rearrange("p (a k) -> p a k", a=2),
             in_=weight.rearrange("(a p) k -> p a k", a=2),
         )
-        load(0, 1)
-        nc.sync.dma_start(out=bias_rows[0:1, :], in_=bias.unsqueeze(0))
-        for piece in range(2, len(LOADS[0])):
+        for piece in range(1, len(LOADS[0])):
             load(0, piece)
         for r in range(1, NXB):
             for piece in range(len(LOADS[r])):
@@ -100,22 +102,23 @@ def tile_bitnetlinear_t_kernel(tc, x, weight, bias, out):
         outs = {}
 
         def open_tiles(s):
-            gr = gpool.tile([P, T * D_IN], BF16, name="gr", tag="gr", align_bytes=64)
+            gr = gpool.tile([P, ROUNDS[s][2] * D_IN], BF16, name="gr", tag="gr", align_bytes=64)
             grouped[s] = gr
 
         def transpose_tiles(s, t_from, t_to):
-            r, t0 = s // RPR, (s % RPR) * T
+            r, t0, n = ROUNDS[s]
             xw = x_tiles[r][:].bitcast(F32)
             gr32 = grouped[s][:].bitcast(F32).rearrange(
-                "p (t g c u) -> p t g c u", t=T, g=2, c=P, u=2
+                "p (t g c u) -> p t g c u", t=n, g=2, c=P, u=2
             )
             for t in range(t_from, t_to):
                 tp = transposes(xw[:, (t0 + t) * WORDS : (t0 + t + 1) * WORDS], "tp")
                 nc.scalar.copy(out=gr32[:, t], in_=tp)
 
         def stage_q(s):
-            cd = cpool.tile([P, T * 2 * P], U32, name="cd", tag="cd", align_bytes=64)
-            sc = cpool.tile([P, T * 2 * P], U8, name="sc", tag="sc", align_bytes=64)
+            n = ROUNDS[s][2]
+            cd = cpool.tile([P, n * 2 * P], U32, name="cd", tag="cd", align_bytes=64)
+            sc = cpool.tile([P, n * 2 * P], U8, name="sc", tag="sc", align_bytes=64)
             nc.vector.quantize_mx(out=cd[:].bitcast(FP8X4), scales=sc[:], in_=grouped[s][:])
             codes[s] = (cd, sc)
 
@@ -128,7 +131,19 @@ def tile_bitnetlinear_t_kernel(tc, x, weight, bias, out):
         w_neg = const.tile([P, 2 * D_IN], BF16, name="w_neg")
 
         open_tiles(0)
-        transpose_tiles(0, 0, 2)
+        transpose_tiles(0, 0, 1)
+        bias_ps = ps_o.tile([P, 512], F32, name="bias_ps", tag="op")
+        for h in range(2):
+            nc.tensor.matmul(
+                out=bias_ps[:, h * D_OUT : (h + 1) * D_OUT],
+                lhsT=ones_bf[:],
+                rhs=bias_rows[:],
+                start=True,
+                stop=True,
+            )
+        bias2 = const.tile([P, 512], F32, name="bias2")
+        nc.vector.tensor_copy(out=bias2[:], in_=bias_ps[:])
+        transpose_tiles(0, 1, 2)
 
         nc.scalar.activation(
             out=w_pos[:, :D_IN], in_=w_sb[:, :D_IN], func=ACT.Abs, accum_out=sum_s[:]
@@ -169,30 +184,19 @@ def tile_bitnetlinear_t_kernel(tc, x, weight, bias, out):
         nc.vector.tensor_scalar(
             out=w_neg[:], in0=wg[:], scalar1=nthr, scalar2=scale, op0=ALU.is_lt, op1=ALU.mult
         )
-        stage_q(0)
         nc.vector.tensor_tensor(out=wq[:], in0=w_pos[:], in1=w_neg[:], op=ALU.subtract)
-        bias_ps = ps_o.tile([P, 512], F32, name="bias_ps", tag="op")
-        for h in range(2):
-            nc.tensor.matmul(
-                out=bias_ps[:, h * D_OUT : (h + 1) * D_OUT],
-                lhsT=ones_bf[:],
-                rhs=bias_rows[:],
-                start=True,
-                stop=True,
-            )
-        bias2 = const.tile([P, 512], F32, name="bias2")
-        nc.vector.tensor_copy(out=bias2[:], in_=bias_ps[:])
+        stage_q(0)
         w_codes = const.tile([P, 2 * D_OUT], U32, name="w_codes", align_bytes=64)
         w_scales = const.tile([P, 2 * D_OUT], U8, name="w_scales", align_bytes=64)
         nc.vector.quantize_mx(out=w_codes[:].bitcast(FP8X4), scales=w_scales[:], in_=wq[:])
 
         def stage_m(s):
-            r, t0 = s // RPR, (s % RPR) * T
+            r, t0, n = ROUNDS[s]
             cd, sc = codes[s]
             if t0 == 0:
                 outs[r] = opool.tile([P, RT * D_OUT], F32, name="osb", tag="osb")
             osb = outs[r]
-            for h in range(T // 2):
+            for h in range(n // 2):
                 op = ps_o.tile([P, 512], F32, name="op", tag="op")
                 for i in range(2):
                     t = 2 * h + i
@@ -213,7 +217,7 @@ def tile_bitnetlinear_t_kernel(tc, x, weight, bias, out):
                     out=osb[:, first : first + 512], in0=op[:], in1=bias2[:], op=ALU.add
                 )
             for s0, s1 in STORES[r]:
-                if s1 == t0 + T:
+                if s1 == t0 + n:
                     nc.sync.dma_start(
                         out=of[r * REGION : (r + 1) * REGION, :].rearrange(
                             "(p t) o -> p t o", t=RT
@@ -224,10 +228,11 @@ def tile_bitnetlinear_t_kernel(tc, x, weight, bias, out):
         for s in range(1, NR + 2):
             if s < NR:
                 open_tiles(s)
-                transpose_tiles(s, 0, T)
-                if (s + 1) % RPR == 0 and (s + 1) // RPR + NXB - 1 < NREG:
-                    for piece in range(len(LOADS[(s + 1) // RPR + NXB - 1])):
-                        load((s + 1) // RPR + NXB - 1, piece)
+                r, t0, n = ROUNDS[s]
+                transpose_tiles(s, 0, n)
+                if t0 + n == RT and r + NXB < NREG:
+                    for piece in range(len(LOADS[r + NXB])):
+                        load(r + NXB, piece)
             if 2 <= s <= NR:
                 stage_q(s - 1)
             if s >= 2:

from contextlib import ExitStack

import concourse.mybir as mybir
from concourse.masks import make_identity

F32 = mybir.dt.float32
BF16 = mybir.dt.bfloat16
U32 = mybir.dt.uint32
U8 = mybir.dt.uint8
FP8X4 = mybir.dt.float8_e4m3fn_x4
ALU = mybir.AluOpType
ACT = mybir.ActivationFunctionType

P = 128
TOKENS = 4 * 2048
D_IN = 1024
D_OUT = 256
FLOPS = 2 * TOKENS * D_IN * D_OUT
WORDS = D_IN // 2

RT = 16
REGION = P * RT
NREG = TOKENS // REGION
T = 4
ROUNDS = [(r, t0, T) for r in range(NREG) for t0 in range(0, RT, T)][:-1] + [
    (NREG - 1, RT - 4, 2),
    (NREG - 1, RT - 2, 2),
]
NR = len(ROUNDS)
LOADS = (
    ((0, 2), (2, 4), (4, 8), (8, 12), (12, 16)),
    ((0, 8), (8, 16)),
    ((0, 8), (8, 16)),
    ((0, 8), (8, 16)),
)
STORES = (((0, 16),), ((0, 16),), ((0, 16),), ((0, 8), (8, 12), (12, 14), (14, 16)))
NXB = 3


def tile_bitnetlinear_t_kernel(tc, x, weight, bias, out):
    nc = tc.nc
    xf = x.flatten_outer_dims()
    of = out.flatten_outer_dims()

    with ExitStack() as ctx:
        const = ctx.enter_context(tc.tile_pool(name="const", bufs=1))
        xpool = ctx.enter_context(tc.tile_pool(name="xin", bufs=NXB))
        gpool = ctx.enter_context(tc.tile_pool(name="grouped", bufs=3))
        cpool = ctx.enter_context(tc.tile_pool(name="codes", bufs=3))
        opool = ctx.enter_context(tc.tile_pool(name="outs", bufs=NREG))
        ps_t = ctx.enter_context(tc.psum_pool(name="ps_t", bufs=4))
        ps_o = ctx.enter_context(tc.psum_pool(name="ps_o", bufs=4))
        ctx.enter_context(tc.manual_schedule())

        x_tiles = {}

        def load(r, piece):
            if piece == 0:
                x_tiles[r] = xpool.tile([P, RT * D_IN], BF16, name="x_sb", tag="x_sb")
            t0, t1 = LOADS[r][piece]
            nc.sync.dma_start(
                out=x_tiles[r][:].rearrange("p (t k) -> p t k", t=RT)[:, t0:t1, :],
                in_=xf[r * REGION : (r + 1) * REGION, :].rearrange("(p t) k -> p t k", t=RT)[
                    :, t0:t1, :
                ],
            )

        bias_rows = const.tile([P, D_OUT], BF16, name="bias_rows")
        nc.vector.memset(bias_rows[:], 0.0)
        w_sb = const.tile([P, 2 * D_IN], BF16, name="w_sb")
        load(0, 0)
        nc.sync.dma_start(out=bias_rows[0:1, :], in_=bias.unsqueeze(0))
        nc.sync.dma_start(
            out=w_sb[:].rearrange("p (a k) -> p a k", a=2),
            in_=weight.rearrange("(a p) k -> p a k", a=2),
        )
        for piece in range(1, len(LOADS[0])):
            load(0, piece)
        for r in range(1, NXB):
            for piece in range(len(LOADS[r])):
                load(r, piece)

        ones_mean = const.tile([P, P], F32, name="ones_mean")
        nc.vector.memset(ones_mean[:], 1.0 / (D_OUT * D_IN))
        ones_bf = const.tile([P, P], BF16, name="ones_bf")
        nc.vector.memset(ones_bf[:], 1.0)
        warm = const.tile([P, 1], F32, name="warm")
        nc.scalar.activation(out=warm[:], in_=ones_mean[:, 0:1], func=ACT.Abs)
        ident = const.tile([P, P], F32, name="ident")
        make_identity(nc, ident[:])

        def transposes(src_words, name):
            tp = ps_t.tile([P, 512], F32, name=name, tag="tp")
            for j in range(4):
                nc.tensor.transpose(
                    tp[:, j * P : (j + 1) * P], src_words[:, j * P : (j + 1) * P], ident[:]
                )
            return tp[:].rearrange("p (g u c) -> p g c u", g=2, u=2, c=P)

        grouped = {}
        codes = {}
        outs = {}

        def open_tiles(s):
            gr = gpool.tile([P, ROUNDS[s][2] * D_IN], BF16, name="gr", tag="gr", align_bytes=64)
            grouped[s] = gr

        def transpose_tiles(s, t_from, t_to):
            r, t0, n = ROUNDS[s]
            xw = x_tiles[r][:].bitcast(F32)
            gr32 = grouped[s][:].bitcast(F32).rearrange(
                "p (t g c u) -> p t g c u", t=n, g=2, c=P, u=2
            )
            for t in range(t_from, t_to):
                tp = transposes(xw[:, (t0 + t) * WORDS : (t0 + t + 1) * WORDS], "tp")
                nc.scalar.copy(out=gr32[:, t], in_=tp)

        def stage_q(s):
            n = ROUNDS[s][2]
            cd = cpool.tile([P, n * 2 * P], U32, name="cd", tag="cd", align_bytes=64)
            sc = cpool.tile([P, n * 2 * P], U8, name="sc", tag="sc", align_bytes=64)
            nc.vector.quantize_mx(out=cd[:].bitcast(FP8X4), scales=sc[:], in_=grouped[s][:])
            codes[s] = (cd, sc)

        ww = w_sb[:].bitcast(F32)
        wg = const.tile([P, 2 * D_IN], BF16, name="wg", align_bytes=64)
        wg32 = wg[:].bitcast(F32).rearrange("p (g a c u) -> p a g c u", g=2, a=2, c=P, u=2)
        sum_s = const.tile([P, 1], F32, name="sum_s")
        sum_v = const.tile([P, 1], F32, name="sum_v")
        w_pos = const.tile([P, 2 * D_IN], BF16, name="w_pos")
        w_neg = const.tile([P, 2 * D_IN], BF16, name="w_neg")

        open_tiles(0)
        transpose_tiles(0, 0, 1)
        bias_ps = ps_o.tile([P, 512], F32, name="bias_ps", tag="op")
        for h in range(2):
            nc.tensor.matmul(
                out=bias_ps[:, h * D_OUT : (h + 1) * D_OUT],
                lhsT=ones_bf[:],
                rhs=bias_rows[:],
                start=True,
                stop=True,
            )
        bias2 = const.tile([P, 512], F32, name="bias2")
        nc.vector.tensor_copy(out=bias2[:], in_=bias_ps[:])
        transpose_tiles(0, 1, 2)

        nc.scalar.activation(
            out=w_pos[:, :D_IN], in_=w_sb[:, :D_IN], func=ACT.Abs, accum_out=sum_s[:]
        )
        nc.vector.tensor_reduce(
            out=sum_v[:],
            in_=w_sb[:, D_IN:],
            axis=mybir.AxisListType.X,
            op=ALU.add,
            apply_absolute_value=True,
        )
        for a in range(2):
            tpw = transposes(ww[:, a * WORDS : (a + 1) * WORDS], "tpw")
            nc.vector.tensor_copy(out=wg32[:, a], in_=tpw)

        mean_ps = ps_o.tile([P, 512], F32, name="mean_ps", tag="op")
        nc.tensor.matmul(
            out=mean_ps[:, 0:1], lhsT=ones_mean[:], rhs=sum_v[:], start=True, stop=False
        )
        nc.tensor.matmul(
            out=mean_ps[:, 0:1], lhsT=ones_mean[:], rhs=sum_s[:], start=False, stop=True
        )
        transpose_tiles(0, 2, T)

        sv = const.tile([P, 4], F32, name="sv")
        scale = sv[:, 0:1]
        thr = sv[:, 1:2]
        nthr = sv[:, 2:3]
        nc.vector.tensor_scalar(
            out=scale, in0=mean_ps[:, 0:1], scalar1=1e-5, scalar2=1000.0, op0=ALU.max, op1=ALU.min
        )
        nc.vector.tensor_scalar(out=thr, in0=scale, scalar1=2.0 / 3.0, scalar2=None, op0=ALU.mult)
        nc.vector.tensor_scalar(out=nthr, in0=scale, scalar1=-2.0 / 3.0, scalar2=None, op0=ALU.mult)
        wq = const.tile([P, 2 * D_IN], BF16, name="wq", align_bytes=64)
        nc.vector.tensor_scalar(
            out=w_pos[:], in0=wg[:], scalar1=thr, scalar2=scale, op0=ALU.is_gt, op1=ALU.mult
        )
        nc.vector.tensor_scalar(
            out=w_neg[:], in0=wg[:], scalar1=nthr, scalar2=scale, op0=ALU.is_lt, op1=ALU.mult
        )
        nc.vector.tensor_tensor(out=wq[:], in0=w_pos[:], in1=w_neg[:], op=ALU.subtract)
        stage_q(0)
        w_codes = const.tile([P, 2 * D_OUT], U32, name="w_codes", align_bytes=64)
        w_scales = const.tile([P, 2 * D_OUT], U8, name="w_scales", align_bytes=64)
        nc.vector.quantize_mx(out=w_codes[:].bitcast(FP8X4), scales=w_scales[:], in_=wq[:])

        def stage_m(s):
            r, t0, n = ROUNDS[s]
            cd, sc = codes[s]
            if t0 == 0:
                outs[r] = opool.tile([P, RT * D_OUT], F32, name="osb", tag="osb")
            osb = outs[r]
            for h in range(n // 2):
                op = ps_o.tile([P, 512], F32, name="op", tag="op")
                for i in range(2):
                    t = 2 * h + i
                    for g in range(2):
                        cols = slice((2 * t + g) * P, (2 * t + g + 1) * P)
                        wcols = slice(g * D_OUT, (g + 1) * D_OUT)
                        nc.tensor.matmul_mx(
                            out=op[:, i * D_OUT : (i + 1) * D_OUT],
                            lhsT=cd[:, cols].bitcast(FP8X4),
                            lhsT_scale=sc[:, cols],
                            rhs=w_codes[:, wcols].bitcast(FP8X4),
                            rhs_scale=w_scales[:, wcols],
                            start=(g == 0),
                            stop=(g == 1),
                        )
                first = (t0 + 2 * h) * D_OUT
                nc.vector.tensor_tensor(
                    out=osb[:, first : first + 512], in0=op[:], in1=bias2[:], op=ALU.add
                )
            for s0, s1 in STORES[r]:
                if s1 == t0 + n:
                    nc.sync.dma_start(
                        out=of[r * REGION : (r + 1) * REGION, :].rearrange(
                            "(p t) o -> p t o", t=RT
                        )[:, s0:s1, :],
                        in_=osb[:].rearrange("p (t o) -> p t o", t=RT)[:, s0:s1, :],
                    )

        for s in range(1, NR + 2):
            if s < NR:
                open_tiles(s)
                r, t0, n = ROUNDS[s]
                transpose_tiles(s, 0, n)
                if t0 + n == RT and r + NXB < NREG:
                    for piece in range(len(LOADS[r + NXB])):
                        load(r + NXB, piece)
            if 2 <= s <= NR:
                stage_q(s - 1)
            if s >= 2:
                stage_m(s - 2)
